import numpy as np
import ml_dtypes


def mxq(x, axis, fmt="e4m3"):
    dtype, down = {"e4m3": (ml_dtypes.float8_e4m3fn, 7), "e5m2": (ml_dtypes.float8_e5m2, 14)}[fmt]
    v = np.moveaxis(np.asarray(x, np.float32).astype(ml_dtypes.bfloat16).astype(np.float64), axis, -1)
    blocks = v.reshape(v.shape[:-1] + (-1, 32))
    amax = np.abs(blocks).max(-1, keepdims=True)
    byte = np.maximum(np.where(amax > 0, np.frexp(amax)[1] - 1 + 127, 0) - down, 1)
    scale = np.exp2(byte - 127.0)
    codes = (blocks / scale).astype(np.float32).astype(dtype).astype(np.float64)
    return np.moveaxis((codes * scale).reshape(v.shape), -1, axis)


WIDE = False


def mx_kscale(k):
    if not WIDE:
        return np.ones(k)
    levels = np.array([10, -10, 5, -5, 0])
    if k % 512:
        return np.exp2(np.random.permutation(np.resize(levels, k // 32))).repeat(32)
    a = np.empty((k // 512, 16))
    for p in range(k // 512):
        a[p, :8] = np.random.permutation(np.resize(levels, 8))
        for g in range(8):
            far = levels[np.abs(levels - a[p, g]) >= 10]
            a[p, g + 8] = far[np.random.randint(len(far))]
    return np.exp2(a.ravel()).repeat(32)


BF16 = ml_dtypes.bfloat16


def bf(x):
    return np.asarray(x, np.float32).astype(BF16)


def f64(x):
    return np.asarray(x).astype(np.float64)


N, E, G, M, H = 512, 1024, 512, 512, 4
HG = H * G


def setup_inputs():
    r = np.random.standard_normal
    s = mx_kscale(M)
    t = mx_kscale(HG)
    return {"h1": bf(np.maximum(r((N, H, M)), 0.0) * s),
            "W2": bf(r((H, M, G)) * 1.5 / np.sqrt(M) / s[None, :, None] * t.reshape(H, 1, G)),
            "b2": bf(r((H, G)) * 0.2 * t.reshape(H, G)),
            "Ws": bf(r((HG, E)) / np.sqrt(HG) / t[:, None]),
            "q": bf(r((N, E))),
            "rep": bf(r((N, E)))}


def reference(h1, W2, b2, Ws, q, rep):
    ht = f64(h1).transpose(1, 0, 2)
    z2 = (mxq(ht, 2, "e4m3") @ mxq(f64(W2), 1, "e4m3")).transpose(1, 0, 2) + f64(b2)
    update_gate = z2.reshape(N, HG)
    return f64(q) - f64(rep) + (mxq(update_gate, 1, "e4m3") @ mxq(f64(Ws), 0, "e4m3"))

@@ -1,0 +1,179 @@
+from contextlib import ExitStack
+
+import concourse.mybir as mybir
+from concourse.masks import make_identity
+
+FP8X4 = mybir.dt.float8_e4m3fn_x4
+BF16 = mybir.dt.bfloat16
+F32 = mybir.dt.float32
+U32 = mybir.dt.uint32
+U8 = mybir.dt.uint8
+ADD = mybir.AluOpType.add
+SUBTRACT = mybir.AluOpType.subtract
+
+P = 128
+PACK = 4
+N, E, G, M, H = 512, 1024, 512, 512, 4
+A = N // P
+N_TILE = 512
+E_HALVES = E // N_TILE
+FLOPS = 2 * N * H * M * G + 2 * N * H * G * E
+
+W2_SHARED_HEADS = (0, 1)
+
+
+def tile_treehopnode_pb_kernel(tc, h1, W2, b2, Ws, q, rep, out):
+    nc = tc.nc
+    with ExitStack() as ctx:
+        sbuf = ctx.enter_context(tc.tile_pool(name="sbuf", bufs=1))
+        psum = ctx.enter_context(tc.psum_pool(name="psum", bufs=1))
+        ctx.enter_context(tc.manual_schedule())
+
+        identity = sbuf.tile([P, P], F32, name="identity")
+        make_identity(nc, identity[:])
+        bias = sbuf.tile([P, H, PACK], BF16, name="bias")
+
+        h1_raw = [sbuf.tile([P, A, M], BF16, name="h1_raw%d" % h) for h in range(H)]
+        w2_raw = [sbuf.tile([P, PACK, G], BF16, name="w2_raw%d" % h) for h in range(H)]
+        ws_raw = [sbuf.tile([P, PACK, E], BF16, name="ws_raw%d" % h) for h in range(H)]
+        q_raw = sbuf.tile([P, A, E], BF16, name="q_raw")
+        rep_raw = sbuf.tile([P, A, E], BF16, name="rep_raw")
+        h1_by_tile = h1.rearrange("(r a) h m -> r a h m", a=A)
+        for h in range(H):
+            nc.sync.dma_start(out=h1_raw[h][:], in_=h1_by_tile[:, :, h, :])
+            nc.sync.dma_start(
+                out=w2_raw[h][:].rearrange("p t g -> p (t g)"),
+                in_=W2[h].rearrange("(p t) g -> p (t g)", t=PACK),
+            )
+            if h == 0:
+                nc.sync.dma_start(out=bias[:], in_=b2.rearrange("h (c t) -> c h t", t=PACK))
+        for h in range(H):
+            nc.sync.dma_start(
+                out=ws_raw[h][:].rearrange("p t e -> p (t e)"),
+                in_=Ws[h * G : (h + 1) * G, :].rearrange("(p t) e -> p (t e)", t=PACK),
+            )
+        nc.sync.dma_start(out=q_raw[:].rearrange("r a e -> r (a e)"), in_=q.rearrange("(r a) e -> r (a e)", a=A))
+        nc.sync.dma_start(out=rep_raw[:].rearrange("r a e -> r (a e)"), in_=rep.rearrange("(r a) e -> r (a e)", a=A))
+
+        def mx_operand(name):
+            return {
+                "grouped": sbuf.tile([P, N_TILE * PACK], BF16, name=name + "_grouped", align_bytes=64),
+                "words": sbuf.tile([P, N_TILE], U32, name=name + "_words", align_bytes=64),
+                "scales": sbuf.tile([P, N_TILE], U8, name=name + "_scales", align_bytes=64),
+            }
+
+        h1_mx = [mx_operand("h1_%d" % h) for h in range(H)]
+        w2_mx = [mx_operand("w2_%d" % h) for h in range(H)]
+        z_mx = [mx_operand("z_%d" % h) for h in range(H)]
+        ws_mx = [[mx_operand("ws_%d_%d" % (half, h)) for h in range(H)] for half in range(E_HALVES)]
+        residual = [sbuf.tile([P, E], F32, name="residual%d" % a) for a in range(A)]
+
+        def quantise(operand):
+            nc.vector.quantize_mx(
+                out=operand["words"][:].bitcast(FP8X4), scales=operand["scales"][:], in_=operand["grouped"][:]
+            )
+
+        def matmul_mx(acc, stationary, moving, stationary_cols, moving_cols, start, stop):
+            nc.tensor.matmul_mx(
+                out=acc,
+                lhsT=stationary["words"][:, stationary_cols].bitcast(FP8X4),
+                lhsT_scale=stationary["scales"][:, stationary_cols],
+                rhs=moving["words"][:, moving_cols].bitcast(FP8X4),
+                rhs_scale=moving["scales"][:, moving_cols],
+                start=start,
+                stop=stop,
+            )
+
+        def psum_bank(shape, bank):
+            return psum.tile(shape, F32, name="bank", tag="bank%d" % bank)
+
+        def prepare_head(h):
+            pairs = h1_raw[h][:].rearrange("r a m -> r (a m)").bitcast(F32)
+            grouped_pairs = h1_mx[h]["grouped"][:].bitcast(F32).rearrange("p (a r u) -> p a r u", a=A, u=2)
+            for b in range(2):
+                bank = psum_bank([P, 2, 2, P], (2 * h + b) % 4)
+                for i in range(2):
+                    for u in range(2):
+                        first = (M // 2) * (2 * b + i)
+                        words = pairs[:, first + u : first + M // 2 : 2]
+                        nc.tensor.transpose(bank[:, i, u, :], words, identity[:])
+                nc.scalar.copy(
+                    out=grouped_pairs[:, 2 * b : 2 * b + 2, :, :], in_=bank[:].rearrange("p i u r -> p i r u")
+                )
+            regrouped = w2_mx[h]["grouped"][:].rearrange("p (t c j) -> p c j t", t=PACK, j=PACK)
+            rows = w2_raw[h][:].rearrange("p j (c t) -> p c j t", t=PACK)
+            scalar_from = P // 2 if h in W2_SHARED_HEADS else 0
+            if scalar_from > 0:
+                nc.vector.tensor_copy(out=regrouped[:, :scalar_from], in_=rows[:, :scalar_from])
+            nc.scalar.copy(out=regrouped[:, scalar_from:], in_=rows[:, scalar_from:])
+
+        def quantise_head(h):
+            quantise(h1_mx[h])
+            quantise(w2_mx[h])
+
+        def stage1(h, a):
+            bank = psum_bank([P, PACK, P], 4 + a)
+            for t in range(PACK):
+                matmul_mx(
+                    bank[:, t, :], w2_mx[h], h1_mx[h], slice(t * P, (t + 1) * P), slice(a * P, (a + 1) * P), True, True
+                )
+            nc.vector.tensor_tensor(
+                out=z_mx[h]["grouped"][:].rearrange("c (a r t) -> c a r t", a=A, t=PACK)[:, a, :, :],
+                in0=bank[:].rearrange("c t r -> c r t"),
+                in1=bias[:, h, :].unsqueeze(1).to_broadcast([P, P, PACK]),
+                op=ADD,
+            )
+
+        def regroup_ws(half, h):
+            nc.scalar.copy(
+                out=ws_mx[half][h]["grouped"][:].rearrange("p (c i t) -> p c t i", i=4, t=PACK),
+                in_=ws_raw[h][:, :, half * N_TILE : (half + 1) * N_TILE].rearrange("p t (c i) -> p c t i", i=4),
+            )
+
+        out_banks = {}
+
+        def stage2(half, h):
+            for a in range(A):
+                if h == 0:
+                    out_banks[(half, a)] = psum_bank([P, N_TILE], 4 * half + a)
+                matmul_mx(
+                    out_banks[(half, a)][:], z_mx[h], ws_mx[half][h], slice(a * P, (a + 1) * P), slice(0, N_TILE),
+                    h == 0, h == H - 1,
+                )
+
+        out_by_tile = out.rearrange("(r a) e -> r a e", a=A)
+
+        def finish(half, a):
+            cols = slice(half * N_TILE, (half + 1) * N_TILE)
+            nc.vector.tensor_tensor(
+                out=residual[a][:, cols], in0=out_banks[(half, a)][:], in1=residual[a][:, cols], op=ADD
+            )
+            nc.sync.dma_start(out=out_by_tile[:, a, cols], in_=residual[a][:, cols])
+
+        prepare_head(0)
+        quantise_head(0)
+        prepare_head(1)
+        for h in range(H):
+            for a in range(A):
+                stage1(h, a)
+                if a == 0 and h > 0:
+                    quantise(z_mx[h - 1])
+                if a == 1 and h + 1 < H:
+                    quantise_head(h + 1)
+                if a == 1 and h + 2 < H:
+                    prepare_head(h + 2)
+
+        for h in range(H):
+            regroup_ws(0, h)
+            quantise(ws_mx[0][h])
+            if h == 0:
+                quantise(z_mx[H - 1])
+            stage2(0, h)
+        for i in range(H):
+            nc.vector.tensor_tensor(out=residual[i][:], in0=q_raw[:, i, :], in1=rep_raw[:, i, :], op=SUBTRACT)
+            regroup_ws(1, i)
+            quantise(ws_mx[1][i])
+            stage2(1, i)
+            finish(0, i)
+        for a in range(A):
+            finish(1, a)

@@ -19,8 +19,6 @@ N_TILE = 512
 E_HALVES = E // N_TILE
 FLOPS = 2 * N * H * M * G + 2 * N * H * G * E
 
-W2_SHARED_HEADS = (0, 1)
-
 
 def tile_treehopnode_pb_kernel(tc, h1, W2, b2, Ws, q, rep, out):
     nc = tc.nc
@@ -31,6 +29,8 @@ def tile_treehopnode_pb_kernel(tc, h1, W2, b2, Ws, q, rep, out):
 
         identity = sbuf.tile([P, P], F32, name="identity")
         make_identity(nc, identity[:])
+        identity_bf16 = sbuf.tile([P, P], BF16, name="identity_bf16")
+        make_identity(nc, identity_bf16[:])
         bias = sbuf.tile([P, H, PACK], BF16, name="bias")
 
         h1_raw = [sbuf.tile([P, A, M], BF16, name="h1_raw%d" % h) for h in range(H)]
@@ -40,13 +40,17 @@ def tile_treehopnode_pb_kernel(tc, h1, W2, b2, Ws, q, rep, out):
         rep_raw = sbuf.tile([P, A, E], BF16, name="rep_raw")
         h1_by_tile = h1.rearrange("(r a) h m -> r a h m", a=A)
         for h in range(H):
-            nc.sync.dma_start(out=h1_raw[h][:], in_=h1_by_tile[:, :, h, :])
             nc.sync.dma_start(
                 out=w2_raw[h][:].rearrange("p t g -> p (t g)"),
                 in_=W2[h].rearrange("(p t) g -> p (t g)", t=PACK),
             )
             if h == 0:
+                for b in range(2):
+                    tiles = slice(2 * b, 2 * b + 2)
+                    nc.sync.dma_start(out=h1_raw[h][:, tiles, :], in_=h1_by_tile[:, tiles, h, :])
                 nc.sync.dma_start(out=bias[:], in_=b2.rearrange("h (c t) -> c h t", t=PACK))
+            else:
+                nc.sync.dma_start(out=h1_raw[h][:], in_=h1_by_tile[:, :, h, :])
         for h in range(H):
             nc.sync.dma_start(
                 out=ws_raw[h][:].rearrange("p t e -> p (t e)"),
@@ -68,9 +72,11 @@ def tile_treehopnode_pb_kernel(tc, h1, W2, b2, Ws, q, rep, out):
         ws_mx = [[mx_operand("ws_%d_%d" % (half, h)) for h in range(H)] for half in range(E_HALVES)]
         residual = [sbuf.tile([P, E], F32, name="residual%d" % a) for a in range(A)]
 
-        def quantise(operand):
+        def quantise(operand, first=0, last=N_TILE):
             nc.vector.quantize_mx(
-                out=operand["words"][:].bitcast(FP8X4), scales=operand["scales"][:], in_=operand["grouped"][:]
+                out=operand["words"][:, first:last].bitcast(FP8X4),
+                scales=operand["scales"][:, first:last],
+                in_=operand["grouped"][:, PACK * first : PACK * last],
             )
 
         def matmul_mx(acc, stationary, moving, stationary_cols, moving_cols, start, stop):
@@ -84,32 +90,65 @@ def tile_treehopnode_pb_kernel(tc, h1, W2, b2, Ws, q, rep, out):
                 stop=stop,
             )
 
-        def psum_bank(shape, bank):
-            return psum.tile(shape, F32, name="bank", tag="bank%d" % bank)
+        def psum_bank(shape, bank, dtype=F32):
+            return psum.tile(shape, dtype, name="bank", tag="bank%d" % bank)
 
-        def prepare_head(h):
+        def transpose_h1(h, first_bank, copies=(nc.scalar.copy, nc.scalar.copy)):
             pairs = h1_raw[h][:].rearrange("r a m -> r (a m)").bitcast(F32)
             grouped_pairs = h1_mx[h]["grouped"][:].bitcast(F32).rearrange("p (a r u) -> p a r u", a=A, u=2)
             for b in range(2):
-                bank = psum_bank([P, 2, 2, P], (2 * h + b) % 4)
+                bank = psum_bank([P, 2, 2, P], first_bank + b)
                 for i in range(2):
                     for u in range(2):
                         first = (M // 2) * (2 * b + i)
                         words = pairs[:, first + u : first + M // 2 : 2]
                         nc.tensor.transpose(bank[:, i, u, :], words, identity[:])
-                nc.scalar.copy(
+                copies[b](
                     out=grouped_pairs[:, 2 * b : 2 * b + 2, :, :], in_=bank[:].rearrange("p i u r -> p i r u")
                 )
-            regrouped = w2_mx[h]["grouped"][:].rearrange("p (t c j) -> p c j t", t=PACK, j=PACK)
-            rows = w2_raw[h][:].rearrange("p j (c t) -> p c j t", t=PACK)
-            scalar_from = P // 2 if h in W2_SHARED_HEADS else 0
-            if scalar_from > 0:
-                nc.vector.tensor_copy(out=regrouped[:, :scalar_from], in_=rows[:, :scalar_from])
-            nc.scalar.copy(out=regrouped[:, scalar_from:], in_=rows[:, scalar_from:])
+
+        def regroup_by_tensor(columns, first_bank):
+            banks = []
+            for b in range(2):
+                bank = psum_bank([P, 2, P, PACK], first_bank + b, BF16)
+                for i in range(2):
+                    nc.tensor.matmul(
+                        bank[:, i, :, :], lhsT=identity_bf16[:], rhs=columns(2 * b + i), start=True, stop=True
+                    )
+                banks.append(bank)
+            return banks
+
+        def copy_regrouped(operand, banks):
+            half = N_TILE * PACK // 2
+            for b in range(2):
+                nc.scalar.copy(
+                    out=operand["grouped"][:, half * b : half * (b + 1)],
+                    in_=banks[b][:].rearrange("p i c t -> p (i c t)"),
+                )
+
+        def w2_columns(h):
+            rows = w2_raw[h][:].rearrange("p j (c t) -> p t c j", t=PACK)
+            return lambda i: rows[:, i, :, :]
+
+        def ws_columns(half, h):
+            rows = ws_raw[h][:].rearrange("p t (e c) -> p e c t", c=P)
+            return lambda i: rows[:, (N_TILE // P) * half + i, :, :]
+
+        def regroup_w2(h, copy):
+            copy(
+                out=w2_mx[h]["grouped"][:].rearrange("p (t c j) -> p c j t", t=PACK, j=PACK),
+                in_=w2_raw[h][:].rearrange("p j (c t) -> p c j t", t=PACK),
+            )
+
+        def regroup_ws(half, h):
+            nc.scalar.copy(
+                out=ws_mx[half][h]["grouped"][:].rearrange("p (c i t) -> p c t i", i=4, t=PACK),
+                in_=ws_raw[h][:, :, half * N_TILE : (half + 1) * N_TILE].rearrange("p t (c i) -> p c t i", i=4),
+            )
 
         def quantise_head(h):
-            quantise(h1_mx[h])
             quantise(w2_mx[h])
+            quantise(h1_mx[h])
 
         def stage1(h, a):
             bank = psum_bank([P, PACK, P], 4 + a)
@@ -124,22 +163,27 @@ def tile_treehopnode_pb_kernel(tc, h1, W2, b2, Ws, q, rep, out):
                 op=ADD,
             )
 
-        def regroup_ws(half, h):
-            nc.scalar.copy(
-                out=ws_mx[half][h]["grouped"][:].rearrange("p (c i t) -> p c t i", i=4, t=PACK),
-                in_=ws_raw[h][:, :, half * N_TILE : (half + 1) * N_TILE].rearrange("p t (c i) -> p c t i", i=4),
-            )
-
         out_banks = {}
 
-        def stage2(half, h):
-            for a in range(A):
-                if h == 0:
-                    out_banks[(half, a)] = psum_bank([P, N_TILE], 4 * half + a)
+        def stage2_tile(a):
+            out_banks[(0, a)] = psum_bank([P, N_TILE], a % 2)
+            for h in range(H):
                 matmul_mx(
-                    out_banks[(half, a)][:], z_mx[h], ws_mx[half][h], slice(a * P, (a + 1) * P), slice(0, N_TILE),
+                    out_banks[(0, a)][:], z_mx[h], ws_mx[0][h], slice(a * P, (a + 1) * P), slice(0, N_TILE),
                     h == 0, h == H - 1,
                 )
+
+        def stage2_pass(h):
+            for a in range(A):
+                if h == 0:
+                    out_banks[(1, a)] = psum_bank([P, N_TILE], 4 + a)
+                matmul_mx(
+                    out_banks[(1, a)][:], z_mx[h], ws_mx[1][h], slice(a * P, (a + 1) * P), slice(0, N_TILE),
+                    h == 0, h == H - 1,
+                )
+
+        def subtract(a):
+            nc.vector.tensor_tensor(out=residual[a][:], in0=q_raw[:, a, :], in1=rep_raw[:, a, :], op=SUBTRACT)
 
         out_by_tile = out.rearrange("(r a) e -> r a e", a=A)
 
@@ -150,30 +194,66 @@ def tile_treehopnode_pb_kernel(tc, h1, W2, b2, Ws, q, rep, out):
             )
             nc.sync.dma_start(out=out_by_tile[:, a, cols], in_=residual[a][:, cols])
 
-        prepare_head(0)
-        quantise_head(0)
-        prepare_head(1)
+        regroup_w2(0, nc.vector.tensor_copy)
+        quantise(w2_mx[0])
+        transpose_h1(0, 0, (nc.scalar.copy, nc.vector.tensor_copy))
+        copy_regrouped(w2_mx[1], regroup_by_tensor(w2_columns(1), 2))
+        quantise(h1_mx[0], 0, N_TILE // 2)
+        quantise(h1_mx[0], N_TILE // 2, N_TILE)
         for h in range(H):
             for a in range(A):
                 stage1(h, a)
-                if a == 0 and h > 0:
+                if h == 0 and a == 1:
+                    transpose_h1(1, 0)
+                if h > 1 and a == 0:
                     quantise(z_mx[h - 1])
-                if a == 1 and h + 1 < H:
+                if a == (1 if h > 0 else 3) and h + 1 < H:
                     quantise_head(h + 1)
-                if a == 1 and h + 2 < H:
-                    prepare_head(h + 2)
-
-        for h in range(H):
-            regroup_ws(0, h)
-            quantise(ws_mx[0][h])
             if h == 0:
-                quantise(z_mx[H - 1])
-            stage2(0, h)
-        for i in range(H):
-            nc.vector.tensor_tensor(out=residual[i][:], in0=q_raw[:, i, :], in1=rep_raw[:, i, :], op=SUBTRACT)
-            regroup_ws(1, i)
-            quantise(ws_mx[1][i])
-            stage2(1, i)
-            finish(0, i)
+                quantise(z_mx[0])
+            if h + 2 < H:
+                regroup_w2(h + 2, nc.scalar.copy)
+                transpose_h1(h + 2, 2 * (1 - h))
+
+        def deliver_ws(half, h, banks=None):
+            if banks is None:
+                regroup_ws(half, h)
+            else:
+                copy_regrouped(ws_mx[half][h], banks)
+
+        by_tensor = regroup_by_tensor(ws_columns(0, 3), 2)
+        deliver_ws(0, 0)
+        deliver_ws(0, 1)
+        deliver_ws(0, 2)
+        deliver_ws(0, 3, by_tensor)
+        by_tensor = regroup_by_tensor(ws_columns(1, 1), 2)
+        deliver_ws(1, 0)
+        deliver_ws(1, 1, by_tensor)
+
+        quantise(ws_mx[0][0])
+        quantise(z_mx[H - 1])
+        quantise(ws_mx[0][1])
+        subtract(0)
+        quantise(ws_mx[0][2])
+        subtract(1)
+        quantise(ws_mx[0][3])
+        subtract(2)
+        for a in range(A):
+            stage2_tile(a)
+            finish(0, a)
+            if a == 1:
+                subtract(3)
+            if a == 2:
+                quantise(ws_mx[1][0])
+        quantise(ws_mx[1][1])
+        by_tensor = regroup_by_tensor(ws_columns(1, 3), 2)
+        deliver_ws(1, 2)
+        deliver_ws(1, 3, by_tensor)
+        stage2_pass(0)
+        stage2_pass(1)
+        quantise(ws_mx[1][2])
+        stage2_pass(2)
+        quantise(ws_mx[1][3])
+        stage2_pass(3)
         for a in range(A):
             finish(1, a)

@@ -30,7 +30,7 @@ def tile_treehopnode_pb_kernel(tc, h1, W2, b2, Ws, q, rep, out):
         identity = sbuf.tile([P, P], F32, name="identity")
         make_identity(nc, identity[:])
         identity_bf16 = sbuf.tile([P, P], BF16, name="identity_bf16")
-        make_identity(nc, identity_bf16[:])
+        nc.scalar.copy(out=identity_bf16[:], in_=identity[:])
         bias = sbuf.tile([P, H, PACK], BF16, name="bias")
 
         h1_raw = [sbuf.tile([P, A, M], BF16, name="h1_raw%d" % h) for h in range(H)]
@@ -107,14 +107,14 @@ def tile_treehopnode_pb_kernel(tc, h1, W2, b2, Ws, q, rep, out):
                     out=grouped_pairs[:, 2 * b : 2 * b + 2, :, :], in_=bank[:].rearrange("p i u r -> p i r u")
                 )
 
-        def regroup_by_tensor(columns, first_bank):
+        def regroup_by_tensor(half, h):
+            rows = ws_raw[h][:].rearrange("p t (e c) -> p e c t", c=P)
             banks = []
             for b in range(2):
-                bank = psum_bank([P, 2, P, PACK], first_bank + b, BF16)
+                bank = psum_bank([P, 2, P, PACK], 2 + b, BF16)
                 for i in range(2):
-                    nc.tensor.matmul(
-                        bank[:, i, :, :], lhsT=identity_bf16[:], rhs=columns(2 * b + i), start=True, stop=True
-                    )
+                    quarter = rows[:, (N_TILE // P) * half + 2 * b + i, :, :]
+                    nc.tensor.matmul(bank[:, i, :, :], lhsT=identity_bf16[:], rhs=quarter, start=True, stop=True)
                 banks.append(bank)
             return banks
 
@@ -125,14 +125,6 @@ def tile_treehopnode_pb_kernel(tc, h1, W2, b2, Ws, q, rep, out):
                     out=operand["grouped"][:, half * b : half * (b + 1)],
                     in_=banks[b][:].rearrange("p i c t -> p (i c t)"),
                 )
-
-        def w2_columns(h):
-            rows = w2_raw[h][:].rearrange("p j (c t) -> p t c j", t=PACK)
-            return lambda i: rows[:, i, :, :]
-
-        def ws_columns(half, h):
-            rows = ws_raw[h][:].rearrange("p t (e c) -> p e c t", c=P)
-            return lambda i: rows[:, (N_TILE // P) * half + i, :, :]
 
         def regroup_w2(h, copy):
             copy(
@@ -197,7 +189,7 @@ def tile_treehopnode_pb_kernel(tc, h1, W2, b2, Ws, q, rep, out):
         regroup_w2(0, nc.vector.tensor_copy)
         quantise(w2_mx[0])
         transpose_h1(0, 0, (nc.scalar.copy, nc.vector.tensor_copy))
-        copy_regrouped(w2_mx[1], regroup_by_tensor(w2_columns(1), 2))
+        regroup_w2(1, nc.scalar.copy)
         quantise(h1_mx[0], 0, N_TILE // 2)
         quantise(h1_mx[0], N_TILE // 2, N_TILE)
         for h in range(H):
@@ -214,21 +206,16 @@ def tile_treehopnode_pb_kernel(tc, h1, W2, b2, Ws, q, rep, out):
             if h + 2 < H:
                 regroup_w2(h + 2, nc.scalar.copy)
                 transpose_h1(h + 2, 2 * (1 - h))
+            if h == 1:
+                by_tensor = regroup_by_tensor(0, 0)
 
-        def deliver_ws(half, h, banks=None):
-            if banks is None:
-                regroup_ws(half, h)
-            else:
-                copy_regrouped(ws_mx[half][h], banks)
-
-        by_tensor = regroup_by_tensor(ws_columns(0, 3), 2)
-        deliver_ws(0, 0)
-        deliver_ws(0, 1)
-        deliver_ws(0, 2)
-        deliver_ws(0, 3, by_tensor)
-        by_tensor = regroup_by_tensor(ws_columns(1, 1), 2)
-        deliver_ws(1, 0)
-        deliver_ws(1, 1, by_tensor)
+        copy_regrouped(ws_mx[0][0], by_tensor)
+        by_tensor = regroup_by_tensor(0, 2)
+        regroup_ws(0, 1)
+        copy_regrouped(ws_mx[0][2], by_tensor)
+        by_tensor = regroup_by_tensor(1, 0)
+        regroup_ws(0, 3)
+        copy_regrouped(ws_mx[1][0], by_tensor)
 
         quantise(ws_mx[0][0])
         quantise(z_mx[H - 1])
@@ -241,19 +228,17 @@ def tile_treehopnode_pb_kernel(tc, h1, W2, b2, Ws, q, rep, out):
         for a in range(A):
             stage2_tile(a)
             finish(0, a)
+            if a == 0:
+                by_tensor = regroup_by_tensor(1, 2)
+                quantise(ws_mx[1][0])
             if a == 1:
                 subtract(3)
-            if a == 2:
-                quantise(ws_mx[1][0])
-        quantise(ws_mx[1][1])
-        by_tensor = regroup_by_tensor(ws_columns(1, 3), 2)
-        deliver_ws(1, 2)
-        deliver_ws(1, 3, by_tensor)
-        stage2_pass(0)
-        stage2_pass(1)
-        quantise(ws_mx[1][2])
-        stage2_pass(2)
-        quantise(ws_mx[1][3])
-        stage2_pass(3)
+        regroup_ws(1, 1)
+        copy_regrouped(ws_mx[1][2], by_tensor)
+        regroup_ws(1, 3)
+        for h in range(H):
+            if h > 0:
+                quantise(ws_mx[1][h])
+            stage2_pass(h)
         for a in range(A):
             finish(1, a)

@@ -29,8 +29,6 @@ def tile_treehopnode_pb_kernel(tc, h1, W2, b2, Ws, q, rep, out):
 
         identity = sbuf.tile([P, P], F32, name="identity")
         make_identity(nc, identity[:])
-        identity_bf16 = sbuf.tile([P, P], BF16, name="identity_bf16")
-        nc.scalar.copy(out=identity_bf16[:], in_=identity[:])
         bias = sbuf.tile([P, H, PACK], BF16, name="bias")
 
         h1_raw = [sbuf.tile([P, A, M], BF16, name="h1_raw%d" % h) for h in range(H)]
@@ -107,25 +105,6 @@ def tile_treehopnode_pb_kernel(tc, h1, W2, b2, Ws, q, rep, out):
                     out=grouped_pairs[:, 2 * b : 2 * b + 2, :, :], in_=bank[:].rearrange("p i u r -> p i r u")
                 )
 
-        def regroup_by_tensor(half, h):
-            rows = ws_raw[h][:].rearrange("p t (e c) -> p e c t", c=P)
-            banks = []
-            for b in range(2):
-                bank = psum_bank([P, 2, P, PACK], 2 + b, BF16)
-                for i in range(2):
-                    quarter = rows[:, (N_TILE // P) * half + 2 * b + i, :, :]
-                    nc.tensor.matmul(bank[:, i, :, :], lhsT=identity_bf16[:], rhs=quarter, start=True, stop=True)
-                banks.append(bank)
-            return banks
-
-        def copy_regrouped(operand, banks):
-            half = N_TILE * PACK // 2
-            for b in range(2):
-                nc.scalar.copy(
-                    out=operand["grouped"][:, half * b : half * (b + 1)],
-                    in_=banks[b][:].rearrange("p i c t -> p (i c t)"),
-                )
-
         def regroup_w2(h, copy):
             copy(
                 out=w2_mx[h]["grouped"][:].rearrange("p (t c j) -> p c j t", t=PACK, j=PACK),
@@ -157,20 +136,12 @@ def tile_treehopnode_pb_kernel(tc, h1, W2, b2, Ws, q, rep, out):
 
         out_banks = {}
 
-        def stage2_tile(a):
-            out_banks[(0, a)] = psum_bank([P, N_TILE], a % 2)
-            for h in range(H):
-                matmul_mx(
-                    out_banks[(0, a)][:], z_mx[h], ws_mx[0][h], slice(a * P, (a + 1) * P), slice(0, N_TILE),
-                    h == 0, h == H - 1,
-                )
-
-        def stage2_pass(h):
+        def stage2(half, h):
             for a in range(A):
                 if h == 0:
-                    out_banks[(1, a)] = psum_bank([P, N_TILE], 4 + a)
+                    out_banks[(half, a)] = psum_bank([P, N_TILE], 4 * half + a)
                 matmul_mx(
-                    out_banks[(1, a)][:], z_mx[h], ws_mx[1][h], slice(a * P, (a + 1) * P), slice(0, N_TILE),
+                    out_banks[(half, a)][:], z_mx[h], ws_mx[half][h], slice(a * P, (a + 1) * P), slice(0, N_TILE),
                     h == 0, h == H - 1,
                 )
 
@@ -206,39 +177,18 @@ def tile_treehopnode_pb_kernel(tc, h1, W2, b2, Ws, q, rep, out):
             if h + 2 < H:
                 regroup_w2(h + 2, nc.scalar.copy)
                 transpose_h1(h + 2, 2 * (1 - h))
-            if h == 1:
-                by_tensor = regroup_by_tensor(0, 0)
 
-        copy_regrouped(ws_mx[0][0], by_tensor)
-        by_tensor = regroup_by_tensor(0, 2)
-        regroup_ws(0, 1)
-        copy_regrouped(ws_mx[0][2], by_tensor)
-        by_tensor = regroup_by_tensor(1, 0)
-        regroup_ws(0, 3)
-        copy_regrouped(ws_mx[1][0], by_tensor)
-
-        quantise(ws_mx[0][0])
-        quantise(z_mx[H - 1])
-        quantise(ws_mx[0][1])
-        subtract(0)
-        quantise(ws_mx[0][2])
-        subtract(1)
-        quantise(ws_mx[0][3])
-        subtract(2)
-        for a in range(A):
-            stage2_tile(a)
-            finish(0, a)
-            if a == 0:
-                by_tensor = regroup_by_tensor(1, 2)
-                quantise(ws_mx[1][0])
-            if a == 1:
-                subtract(3)
-        regroup_ws(1, 1)
-        copy_regrouped(ws_mx[1][2], by_tensor)
-        regroup_ws(1, 3)
         for h in range(H):
-            if h > 0:
-                quantise(ws_mx[1][h])
-            stage2_pass(h)
+            regroup_ws(0, h)
+            quantise(ws_mx[0][h])
+            if h == 0:
+                quantise(z_mx[H - 1])
+            stage2(0, h)
+        for i in range(H):
+            subtract(i)
+            regroup_ws(1, i)
+            quantise(ws_mx[1][i])
+            stage2(1, i)
+            finish(0, i)
         for a in range(A):
             finish(1, a)

@@ -16,7 +16,7 @@ PACK = 4
 N, E, G, M, H = 512, 1024, 512, 512, 4
 A = N // P
 N_TILE = 512
-E_HALVES = E // N_TILE
+COLUMN_GROUPS = ((0, 512), (512, 256), (768, 256))
 FLOPS = 2 * N * H * M * G + 2 * N * H * G * E
 
 
@@ -57,20 +57,24 @@ def tile_treehopnode_pb_kernel(tc, h1, W2, b2, Ws, q, rep, out):
         nc.sync.dma_start(out=q_raw[:].rearrange("r a e -> r (a e)"), in_=q.rearrange("(r a) e -> r (a e)", a=A))
         nc.sync.dma_start(out=rep_raw[:].rearrange("r a e -> r (a e)"), in_=rep.rearrange("(r a) e -> r (a e)", a=A))
 
-        def mx_operand(name):
+        def mx_operand(name, width=512):
             return {
-                "grouped": sbuf.tile([P, N_TILE * PACK], BF16, name=name + "_grouped", align_bytes=64),
-                "words": sbuf.tile([P, N_TILE], U32, name=name + "_words", align_bytes=64),
-                "scales": sbuf.tile([P, N_TILE], U8, name=name + "_scales", align_bytes=64),
+                "width": width,
+                "grouped": sbuf.tile([P, width * PACK], BF16, name=name + "_grouped", align_bytes=64),
+                "words": sbuf.tile([P, width], U32, name=name + "_words", align_bytes=64),
+                "scales": sbuf.tile([P, width], U8, name=name + "_scales", align_bytes=64),
             }
 
         h1_mx = [mx_operand("h1_%d" % h) for h in range(H)]
         w2_mx = [mx_operand("w2_%d" % h) for h in range(H)]
         z_mx = [mx_operand("z_%d" % h) for h in range(H)]
-        ws_mx = [[mx_operand("ws_%d_%d" % (half, h)) for h in range(H)] for half in range(E_HALVES)]
+        ws_mx = [
+            [mx_operand("ws_%d_%d" % (first, h), width) for h in range(H)] for first, width in COLUMN_GROUPS
+        ]
         residual = [sbuf.tile([P, E], F32, name="residual%d" % a) for a in range(A)]
 
-        def quantise(operand, first=0, last=N_TILE):
+        def quantise(operand, first=0, last=None):
+            last = operand["width"] if last is None else last
             nc.vector.quantize_mx(
                 out=operand["words"][:, first:last].bitcast(FP8X4),
                 scales=operand["scales"][:, first:last],
@@ -91,7 +95,7 @@ def tile_treehopnode_pb_kernel(tc, h1, W2, b2, Ws, q, rep, out):
         def psum_bank(shape, bank, dtype=F32):
             return psum.tile(shape, dtype, name="bank", tag="bank%d" % bank)
 
-        def transpose_h1(h, first_bank, copies=(nc.scalar.copy, nc.scalar.copy)):
+        def transpose_h1(h, first_bank):
             pairs = h1_raw[h][:].rearrange("r a m -> r (a m)").bitcast(F32)
             grouped_pairs = h1_mx[h]["grouped"][:].bitcast(F32).rearrange("p (a r u) -> p a r u", a=A, u=2)
             for b in range(2):
@@ -101,7 +105,7 @@ def tile_treehopnode_pb_kernel(tc, h1, W2, b2, Ws, q, rep, out):
                         first = (M // 2) * (2 * b + i)
                         words = pairs[:, first + u : first + M // 2 : 2]
                         nc.tensor.transpose(bank[:, i, u, :], words, identity[:])
-                copies[b](
+                nc.scalar.copy(
                     out=grouped_pairs[:, 2 * b : 2 * b + 2, :, :], in_=bank[:].rearrange("p i u r -> p i r u")
                 )
 
@@ -111,15 +115,9 @@ def tile_treehopnode_pb_kernel(tc, h1, W2, b2, Ws, q, rep, out):
                 in_=w2_raw[h][:].rearrange("p j (c t) -> p c j t", t=PACK),
             )
 
-        def regroup_ws(half, h):
-            nc.scalar.copy(
-                out=ws_mx[half][h]["grouped"][:].rearrange("p (c i t) -> p c t i", i=4, t=PACK),
-                in_=ws_raw[h][:, :, half * N_TILE : (half + 1) * N_TILE].rearrange("p t (c i) -> p c t i", i=4),
-            )
-
-        def quantise_head(h):
-            quantise(w2_mx[h])
-            quantise(h1_mx[h])
+        def prepare_head(h, first_bank):
+            regroup_w2(h, nc.scalar.copy)
+            transpose_h1(h, first_bank)
 
         def stage1(h, a):
             bank = psum_bank([P, PACK, P], 4 + a)
@@ -134,14 +132,22 @@ def tile_treehopnode_pb_kernel(tc, h1, W2, b2, Ws, q, rep, out):
                 op=ADD,
             )
 
+        def regroup_ws(g, h):
+            first, width = COLUMN_GROUPS[g]
+            nc.scalar.copy(
+                out=ws_mx[g][h]["grouped"][:].rearrange("p (c i t) -> p c t i", i=4, t=PACK),
+                in_=ws_raw[h][:, :, first : first + width].rearrange("p t (c i) -> p c t i", i=4),
+            )
+
         out_banks = {}
 
-        def stage2(half, h):
+        def stage2(g, h):
+            width = COLUMN_GROUPS[g][1]
             for a in range(A):
                 if h == 0:
-                    out_banks[(half, a)] = psum_bank([P, N_TILE], 4 * half + a)
+                    out_banks[(g, a)] = psum_bank([P, width], 4 * (g % 2) + a)
                 matmul_mx(
-                    out_banks[(half, a)][:], z_mx[h], ws_mx[half][h], slice(a * P, (a + 1) * P), slice(0, N_TILE),
+                    out_banks[(g, a)][:], z_mx[h], ws_mx[g][h], slice(a * P, (a + 1) * P), slice(0, width),
                     h == 0, h == H - 1,
                 )
 
@@ -150,45 +156,62 @@ def tile_treehopnode_pb_kernel(tc, h1, W2, b2, Ws, q, rep, out):
 
         out_by_tile = out.rearrange("(r a) e -> r a e", a=A)
 
-        def finish(half, a):
-            cols = slice(half * N_TILE, (half + 1) * N_TILE)
+        def finish(g, a):
+            first, width = COLUMN_GROUPS[g]
+            cols = slice(first, first + width)
             nc.vector.tensor_tensor(
-                out=residual[a][:, cols], in0=out_banks[(half, a)][:], in1=residual[a][:, cols], op=ADD
+                out=residual[a][:, cols], in0=out_banks[(g, a)][:], in1=residual[a][:, cols], op=ADD
             )
             nc.sync.dma_start(out=out_by_tile[:, a, cols], in_=residual[a][:, cols])
 
         regroup_w2(0, nc.vector.tensor_copy)
         quantise(w2_mx[0])
-        transpose_h1(0, 0, (nc.scalar.copy, nc.vector.tensor_copy))
-        regroup_w2(1, nc.scalar.copy)
+        transpose_h1(0, 0)
         quantise(h1_mx[0], 0, N_TILE // 2)
         quantise(h1_mx[0], N_TILE // 2, N_TILE)
-        for h in range(H):
-            for a in range(A):
-                stage1(h, a)
-                if h == 0 and a == 1:
-                    transpose_h1(1, 0)
-                if h > 1 and a == 0:
+        regroup_w2(1, nc.scalar.copy)
+        stage1(0, 0)
+        stage1(0, 1)
+        transpose_h1(1, 0)
+        stage1(0, 2)
+        stage1(0, 3)
+        quantise(w2_mx[1])
+        quantise(h1_mx[1])
+        quantise(z_mx[0])
+        prepare_head(2, 2)
+        for h in range(1, H):
+            stage1(h, 0)
+            stage1(h, 1)
+            if h + 1 < H:
+                quantise(w2_mx[h + 1])
+                if h > 1:
                     quantise(z_mx[h - 1])
-                if a == (1 if h > 0 else 3) and h + 1 < H:
-                    quantise_head(h + 1)
-            if h == 0:
-                quantise(z_mx[0])
+                quantise(h1_mx[h + 1])
+            else:
+                quantise(z_mx[h - 1])
+                regroup_ws(0, 0)
+                quantise(ws_mx[0][0])
+            stage1(h, 2)
+            stage1(h, 3)
             if h + 2 < H:
-                regroup_w2(h + 2, nc.scalar.copy)
-                transpose_h1(h + 2, 2 * (1 - h))
+                prepare_head(h + 2, 0)
 
         for h in range(H):
-            regroup_ws(0, h)
-            quantise(ws_mx[0][h])
-            if h == 0:
+            if h > 0:
+                regroup_ws(0, h)
+                quantise(ws_mx[0][h])
+                subtract(h - 1)
+            if h == 1:
                 quantise(z_mx[H - 1])
-            stage2(0, h)
-        for i in range(H):
-            subtract(i)
-            regroup_ws(1, i)
-            quantise(ws_mx[1][i])
-            stage2(1, i)
-            finish(0, i)
+                stage2(0, 0)
+            if h > 0:
+                stage2(0, h)
+        subtract(A - 1)
+        for g in range(1, len(COLUMN_GROUPS)):
+            for h in range(H):
+                regroup_ws(g, h)
+                quantise(ws_mx[g][h])
+                stage2(g, h)
+                finish(g - 1, h)
         for a in range(A):
-            finish(1, a)
+            finish(len(COLUMN_GROUPS) - 1, a)

@@ -54,8 +54,11 @@ def tile_treehopnode_pb_kernel(tc, h1, W2, b2, Ws, q, rep, out):
                 out=ws_raw[h][:].rearrange("p t e -> p (t e)"),
                 in_=Ws[h * G : (h + 1) * G, :].rearrange("(p t) e -> p (t e)", t=PACK),
             )
-        nc.sync.dma_start(out=q_raw[:].rearrange("r a e -> r (a e)"), in_=q.rearrange("(r a) e -> r (a e)", a=A))
-        nc.sync.dma_start(out=rep_raw[:].rearrange("r a e -> r (a e)"), in_=rep.rearrange("(r a) e -> r (a e)", a=A))
+        q_by_tile = q.rearrange("(r a) e -> r a e", a=A)
+        rep_by_tile = rep.rearrange("(r a) e -> r a e", a=A)
+        for a in range(A):
+            nc.sync.dma_start(out=q_raw[:, a, :], in_=q_by_tile[:, a, :])
+            nc.sync.dma_start(out=rep_raw[:, a, :], in_=rep_by_tile[:, a, :])
 
         def mx_operand(name, width=512):
             return {
@@ -166,15 +169,16 @@ def tile_treehopnode_pb_kernel(tc, h1, W2, b2, Ws, q, rep, out):
 
         regroup_w2(0, nc.vector.tensor_copy)
         quantise(w2_mx[0])
+        warm_up = psum_bank([P, P], 0)
+        for i in range(4):
+            nc.tensor.matmul(warm_up[:], lhsT=identity[:], rhs=identity[:], start=True, stop=True)
         transpose_h1(0, 0)
         quantise(h1_mx[0], 0, N_TILE // 2)
         quantise(h1_mx[0], N_TILE // 2, N_TILE)
         regroup_w2(1, nc.scalar.copy)
-        stage1(0, 0)
-        stage1(0, 1)
+        for a in range(A):
+            stage1(0, a)
         transpose_h1(1, 0)
-        stage1(0, 2)
-        stage1(0, 3)
         quantise(w2_mx[1])
         quantise(h1_mx[1])
         quantise(z_mx[0])
@@ -196,22 +200,23 @@ def tile_treehopnode_pb_kernel(tc, h1, W2, b2, Ws, q, rep, out):
             if h + 2 < H:
                 prepare_head(h + 2, 0)
 
-        for h in range(H):
-            if h > 0:
-                regroup_ws(0, h)
-                quantise(ws_mx[0][h])
-                subtract(h - 1)
-            if h == 1:
-                quantise(z_mx[H - 1])
-                stage2(0, 0)
-            if h > 0:
-                stage2(0, h)
-        subtract(A - 1)
+        regroup_ws(0, 1)
+        quantise(ws_mx[0][1])
+        quantise(z_mx[H - 1])
+        stage2(0, 0)
+        stage2(0, 1)
+        for h in range(2, H):
+            regroup_ws(0, h)
+            quantise(ws_mx[0][h])
+            stage2(0, h)
+        subtract(0)
         for g in range(1, len(COLUMN_GROUPS)):
             for h in range(H):
                 regroup_ws(g, h)
                 quantise(ws_mx[g][h])
                 stage2(g, h)
+                if g == 1 and h + 1 < A:
+                    subtract(h + 1)
                 finish(g - 1, h)
         for a in range(A):
             finish(len(COLUMN_GROUPS) - 1, a)

@@ -29,7 +29,13 @@ def tile_treehopnode_pb_kernel(tc, h1, W2, b2, Ws, q, rep, out):
 
         identity = sbuf.tile([P, P], F32, name="identity")
         make_identity(nc, identity[:])
+        identity_bf16 = sbuf.tile([P, P], BF16, name="identity_bf16")
+        nc.scalar.copy(out=identity_bf16[:], in_=identity[:])
+        minus_identity = sbuf.tile([P, P], BF16, name="minus_identity")
+        nc.scalar.mul(out=minus_identity[:], in_=identity[:], mul=-1.0)
         bias = sbuf.tile([P, H, PACK], BF16, name="bias")
+        bias_rows = sbuf.tile([P, G], BF16, name="bias_rows")
+        nc.vector.memset(bias_rows[:], 0.0)
 
         h1_raw = [sbuf.tile([P, A, M], BF16, name="h1_raw%d" % h) for h in range(H)]
         w2_raw = [sbuf.tile([P, PACK, G], BF16, name="w2_raw%d" % h) for h in range(H)]
@@ -46,7 +52,7 @@ def tile_treehopnode_pb_kernel(tc, h1, W2, b2, Ws, q, rep, out):
                 for b in range(2):
                     tiles = slice(2 * b, 2 * b + 2)
                     nc.sync.dma_start(out=h1_raw[h][:, tiles, :], in_=h1_by_tile[:, tiles, h, :])
-                nc.sync.dma_start(out=bias[:], in_=b2.rearrange("h (c t) -> c h t", t=PACK))
+                nc.sync.dma_start(out=bias_rows[:H, :], in_=b2)
             else:
                 nc.sync.dma_start(out=h1_raw[h][:], in_=h1_by_tile[:, :, h, :])
         for h in range(H):
@@ -56,9 +62,10 @@ def tile_treehopnode_pb_kernel(tc, h1, W2, b2, Ws, q, rep, out):
             )
         q_by_tile = q.rearrange("(r a) e -> r a e", a=A)
         rep_by_tile = rep.rearrange("(r a) e -> r a e", a=A)
-        for a in range(A):
-            nc.sync.dma_start(out=q_raw[:, a, :], in_=q_by_tile[:, a, :])
-            nc.sync.dma_start(out=rep_raw[:, a, :], in_=rep_by_tile[:, a, :])
+        for b in range(2):
+            tiles = slice(2 * b, 2 * b + 2)
+            nc.sync.dma_start(out=q_raw[:, tiles, :], in_=q_by_tile[:, tiles, :])
+            nc.sync.dma_start(out=rep_raw[:, tiles, :], in_=rep_by_tile[:, tiles, :])
 
         def mx_operand(name, width=512):
             return {
@@ -112,11 +119,20 @@ def tile_treehopnode_pb_kernel(tc, h1, W2, b2, Ws, q, rep, out):
                     out=grouped_pairs[:, 2 * b : 2 * b + 2, :, :], in_=bank[:].rearrange("p i u r -> p i r u")
                 )
 
-        def regroup_w2(h, copy):
-            copy(
-                out=w2_mx[h]["grouped"][:].rearrange("p (t c j) -> p c j t", t=PACK, j=PACK),
-                in_=w2_raw[h][:].rearrange("p j (c t) -> p c j t", t=PACK),
+        def transpose_bias(bank):
+            pairs = bias_rows[:].bitcast(F32)
+            turned = psum_bank([P, 2, P], bank)
+            for u in range(2):
+                nc.tensor.transpose(turned[:, u, :], pairs[:, u::2], identity[:])
+            nc.scalar.copy(
+                out=bias[:].rearrange("c h t -> c (h t)").bitcast(F32).rearrange("c (h u) -> c h u", u=2),
+                in_=turned[:, :, :H].rearrange("c u h -> c h u"),
             )
+
+        def regroup_w2(h, copy, first=0, last=P):
+            regrouped = w2_mx[h]["grouped"][:].rearrange("p (t c j) -> p c j t", t=PACK, j=PACK)
+            rows = w2_raw[h][:].rearrange("p j (c t) -> p c j t", t=PACK)
+            copy(out=regrouped[:, first:last], in_=rows[:, first:last])
 
         def prepare_head(h, first_bank):
             regroup_w2(h, nc.scalar.copy)
@@ -157,6 +173,20 @@ def tile_treehopnode_pb_kernel(tc, h1, W2, b2, Ws, q, rep, out):
         def subtract(a):
             nc.vector.tensor_tensor(out=residual[a][:], in0=q_raw[:, a, :], in1=rep_raw[:, a, :], op=SUBTRACT)
 
+        def subtract_by_tensor(a, first_bank):
+            banks = []
+            for c in range(2):
+                cols = slice(N_TILE * c, N_TILE * (c + 1))
+                bank = psum_bank([P, N_TILE], first_bank + c)
+                nc.tensor.matmul(bank[:], lhsT=identity_bf16[:], rhs=q_raw[:, a, cols], start=True, stop=False)
+                nc.tensor.matmul(bank[:], lhsT=minus_identity[:], rhs=rep_raw[:, a, cols], start=False, stop=True)
+                banks.append(bank)
+            return banks
+
+        def copy_residual(a, banks):
+            for c in range(2):
+                nc.scalar.copy(out=residual[a][:, N_TILE * c : N_TILE * (c + 1)], in_=banks[c][:])
+
         out_by_tile = out.rearrange("(r a) e -> r a e", a=A)
 
         def finish(g, a):
@@ -167,12 +197,14 @@ def tile_treehopnode_pb_kernel(tc, h1, W2, b2, Ws, q, rep, out):
             )
             nc.sync.dma_start(out=out_by_tile[:, a, cols], in_=residual[a][:, cols])
 
-        regroup_w2(0, nc.vector.tensor_copy)
+        regroup_w2(0, nc.vector.tensor_copy, 0, P // 2)
+        regroup_w2(0, nc.scalar.copy, P // 2, P)
         quantise(w2_mx[0])
         warm_up = psum_bank([P, P], 0)
         for i in range(4):
             nc.tensor.matmul(warm_up[:], lhsT=identity[:], rhs=identity[:], start=True, stop=True)
         transpose_h1(0, 0)
+        transpose_bias(2)
         quantise(h1_mx[0], 0, N_TILE // 2)
         quantise(h1_mx[0], N_TILE // 2, N_TILE)
         regroup_w2(1, nc.scalar.copy)
@@ -205,18 +237,37 @@ def tile_treehopnode_pb_kernel(tc, h1, W2, b2, Ws, q, rep, out):
         quantise(z_mx[H - 1])
         stage2(0, 0)
         stage2(0, 1)
-        for h in range(2, H):
-            regroup_ws(0, h)
-            quantise(ws_mx[0][h])
-            stage2(0, h)
-        subtract(0)
-        for g in range(1, len(COLUMN_GROUPS)):
+        banks0 = subtract_by_tensor(0, 4)
+        regroup_ws(0, 2)
+        quantise(ws_mx[0][2])
+        stage2(0, 2)
+        regroup_ws(0, 3)
+        quantise(ws_mx[0][3])
+        stage2(0, 3)
+        regroup_ws(1, 0)
+        quantise(ws_mx[1][0])
+        copy_residual(0, banks0)
+        subtract(1)
+        subtract(2)
+        regroup_ws(1, 1)
+        quantise(ws_mx[1][1])
+        subtract(3)
+        finish(0, 0)
+        regroup_ws(1, 2)
+        quantise(ws_mx[1][2])
+        finish(0, 1)
+        finish(0, 2)
+        for h in range(3):
+            stage2(1, h)
+        regroup_ws(1, 3)
+        quantise(ws_mx[1][3])
+        stage2(1, 3)
+        finish(0, 3)
+        for g in range(2, len(COLUMN_GROUPS)):
             for h in range(H):
                 regroup_ws(g, h)
                 quantise(ws_mx[g][h])
                 stage2(g, h)
-                if g == 1 and h + 1 < A:
-                    subtract(h + 1)
                 finish(g - 1, h)
         for a in range(A):
             finish(len(COLUMN_GROUPS) - 1, a)

@@ -10,6 +10,9 @@ U32 = mybir.dt.uint32
 U8 = mybir.dt.uint8
 ADD = mybir.AluOpType.add
 SUBTRACT = mybir.AluOpType.subtract
+MULT = mybir.AluOpType.mult
+HEADS = 2
+W2_VECTOR = 80
 
 P = 128
 PACK = 4
@@ -37,58 +40,70 @@ def tile_treehopnode_pb_kernel(tc, h1, W2, b2, Ws, q, rep, out):
         bias_rows = sbuf.tile([P, G], BF16, name="bias_rows")
         nc.vector.memset(bias_rows[:], 0.0)
 
-        h1_raw = [sbuf.tile([P, A, M], BF16, name="h1_raw%d" % h) for h in range(H)]
+        h1_raw = [sbuf.tile([P, A, HEADS * M], BF16, name="h1_raw%d" % x) for x in range(H // HEADS)]
         w2_raw = [sbuf.tile([P, PACK, G], BF16, name="w2_raw%d" % h) for h in range(H)]
         ws_raw = [sbuf.tile([P, PACK, E], BF16, name="ws_raw%d" % h) for h in range(H)]
         q_raw = sbuf.tile([P, A, E], BF16, name="q_raw")
         rep_raw = sbuf.tile([P, A, E], BF16, name="rep_raw")
-        h1_by_tile = h1.rearrange("(r a) h m -> r a h m", a=A)
-        for h in range(H):
+        h1_by_tile = h1.rearrange("(r a) (x i) m -> x r a (i m)", a=A, i=HEADS)
+        q_by_tile = q.rearrange("(r a) e -> r a e", a=A)
+        rep_by_tile = rep.rearrange("(r a) e -> r a e", a=A)
+
+        def load_h1(x, first, last):
+            nc.sync.dma_start(out=h1_raw[x][:, first:last, :], in_=h1_by_tile[x, :, first:last, :])
+
+        def load_w2(h):
             nc.sync.dma_start(
                 out=w2_raw[h][:].rearrange("p t g -> p (t g)"),
                 in_=W2[h].rearrange("(p t) g -> p (t g)", t=PACK),
             )
-            if h == 0:
-                for b in range(2):
-                    tiles = slice(2 * b, 2 * b + 2)
-                    nc.sync.dma_start(out=h1_raw[h][:, tiles, :], in_=h1_by_tile[:, tiles, h, :])
-                nc.sync.dma_start(out=bias_rows[:H, :], in_=b2)
-            else:
-                nc.sync.dma_start(out=h1_raw[h][:], in_=h1_by_tile[:, :, h, :])
-        for h in range(H):
+
+        def load_ws(h):
             nc.sync.dma_start(
                 out=ws_raw[h][:].rearrange("p t e -> p (t e)"),
                 in_=Ws[h * G : (h + 1) * G, :].rearrange("(p t) e -> p (t e)", t=PACK),
             )
-        q_by_tile = q.rearrange("(r a) e -> r a e", a=A)
-        rep_by_tile = rep.rearrange("(r a) e -> r a e", a=A)
+
+        load_w2(0)
+        load_h1(0, 0, 1)
+        load_h1(0, 1, 2)
+        nc.sync.dma_start(out=bias_rows[:H, :], in_=b2)
+        load_w2(1)
+        load_h1(0, 2, 4)
+        load_w2(2)
+        load_h1(1, 0, 2)
+        load_h1(1, 2, 4)
+        load_w2(3)
+        for h in range(H):
+            load_ws(h)
         for b in range(2):
             tiles = slice(2 * b, 2 * b + 2)
             nc.sync.dma_start(out=q_raw[:, tiles, :], in_=q_by_tile[:, tiles, :])
             nc.sync.dma_start(out=rep_raw[:, tiles, :], in_=rep_by_tile[:, tiles, :])
 
-        def mx_operand(name, width=512):
+        def mx_operand(name, width=512, grouped=True):
             return {
                 "width": width,
-                "grouped": sbuf.tile([P, width * PACK], BF16, name=name + "_grouped", align_bytes=64),
+                "grouped": sbuf.tile([P, width * PACK], BF16, name=name + "_grouped", align_bytes=64) if grouped else None,
                 "words": sbuf.tile([P, width], U32, name=name + "_words", align_bytes=64),
                 "scales": sbuf.tile([P, width], U8, name=name + "_scales", align_bytes=64),
             }
 
-        h1_mx = [mx_operand("h1_%d" % h) for h in range(H)]
-        w2_mx = [mx_operand("w2_%d" % h) for h in range(H)]
+        h1_mx = [mx_operand("h1_%d" % x, A * HEADS * P) for x in range(H // HEADS)]
+        w2_mx = [mx_operand("w2_%d" % h, grouped=h == 0) for h in range(H)]
         z_mx = [mx_operand("z_%d" % h) for h in range(H)]
         ws_mx = [
             [mx_operand("ws_%d_%d" % (first, h), width) for h in range(H)] for first, width in COLUMN_GROUPS
         ]
         residual = [sbuf.tile([P, E], F32, name="residual%d" % a) for a in range(A)]
 
-        def quantise(operand, first=0, last=None):
+        def quantise(operand, first=0, last=None, source=None):
             last = operand["width"] if last is None else last
+            source = operand["grouped"][:, PACK * first : PACK * last] if source is None else source
             nc.vector.quantize_mx(
                 out=operand["words"][:, first:last].bitcast(FP8X4),
                 scales=operand["scales"][:, first:last],
-                in_=operand["grouped"][:, PACK * first : PACK * last],
+                in_=source,
             )
 
         def matmul_mx(acc, stationary, moving, stationary_cols, moving_cols, start, stop):
@@ -105,19 +120,18 @@ def tile_treehopnode_pb_kernel(tc, h1, W2, b2, Ws, q, rep, out):
         def psum_bank(shape, bank, dtype=F32):
             return psum.tile(shape, dtype, name="bank", tag="bank%d" % bank)
 
-        def transpose_h1(h, first_bank):
-            pairs = h1_raw[h][:].rearrange("r a m -> r (a m)").bitcast(F32)
-            grouped_pairs = h1_mx[h]["grouped"][:].bitcast(F32).rearrange("p (a r u) -> p a r u", a=A, u=2)
-            for b in range(2):
-                bank = psum_bank([P, 2, 2, P], first_bank + b)
-                for i in range(2):
-                    for u in range(2):
-                        first = (M // 2) * (2 * b + i)
-                        words = pairs[:, first + u : first + M // 2 : 2]
-                        nc.tensor.transpose(bank[:, i, u, :], words, identity[:])
-                nc.scalar.copy(
-                    out=grouped_pairs[:, 2 * b : 2 * b + 2, :, :], in_=bank[:].rearrange("p i u r -> p i r u")
-                )
+        def transpose_h1(x, a, b):
+            pairs = h1_raw[x][:].rearrange("r a m -> r (a m)").bitcast(F32)
+            bank = psum_bank([P, HEADS, 2, P], b)
+            for i in range(HEADS):
+                for u in range(2):
+                    first = (M // 2) * (HEADS * a + i)
+                    nc.tensor.transpose(bank[:, i, u, :], pairs[:, first + u : first + M // 2 : 2], identity[:])
+            return bank
+
+        def copy_h1(x, a, bank):
+            grouped_pairs = h1_mx[x]["grouped"][:].bitcast(F32).rearrange("p (a i r u) -> p a i r u", a=A, i=HEADS, u=2)
+            nc.scalar.copy(out=grouped_pairs[:, a], in_=bank[:].rearrange("p i u r -> p i r u"))
 
         def transpose_bias(bank):
             pairs = bias_rows[:].bitcast(F32)
@@ -129,21 +143,46 @@ def tile_treehopnode_pb_kernel(tc, h1, W2, b2, Ws, q, rep, out):
                 in_=turned[:, :, :H].rearrange("c u h -> c h u"),
             )
 
+        def copy_by_gpsimd(out, in_):
+            nc.gpsimd.tensor_scalar(out=out, in0=in_, scalar1=1.0, scalar2=0.0, op0=MULT, op1=ADD)
+
         def regroup_w2(h, copy, first=0, last=P):
             regrouped = w2_mx[h]["grouped"][:].rearrange("p (t c j) -> p c j t", t=PACK, j=PACK)
             rows = w2_raw[h][:].rearrange("p j (c t) -> p c j t", t=PACK)
             copy(out=regrouped[:, first:last], in_=rows[:, first:last])
 
-        def prepare_head(h, first_bank):
-            regroup_w2(h, nc.scalar.copy)
-            transpose_h1(h, first_bank)
+        def regroup_w2_shared(h, split, tag="w2_shared"):
+            w2_mx[h]["grouped"] = sbuf.tile([P, N_TILE * PACK], BF16, name="w2_shared", tag=tag, align_bytes=64)
+            regrouped = w2_mx[h]["grouped"][:].rearrange("p (t c j) -> p t c j", t=PACK, j=PACK)
+            rows = w2_raw[h][:].rearrange("p j (c t) -> p t c j", t=PACK)
+            for t in range(split, PACK):
+                copy_by_gpsimd(regrouped[:, t], rows[:, t])
+            nc.scalar.copy(
+                out=regrouped[:, :split].rearrange("p t c j -> p c j t"), in_=rows[:, :split].rearrange("p t c j -> p c j t")
+            )
 
-        def stage1(h, a):
-            bank = psum_bank([P, PACK, P], 4 + a)
+        def regroup_ws_by_gpsimd(pieces):
+            tile = sbuf.tile([P, N_TILE * PACK], BF16, name="w2_shared", tag="w2_shared", align_bytes=64)
+            at = 0
+            for g, h, first, width in pieces:
+                for k in range(0, width, P):
+                    out = tile[:, PACK * at : PACK * (at + P)].rearrange("p (c t) -> p c t", t=PACK)
+                    lo = COLUMN_GROUPS[g][0] + first + k
+                    copy_by_gpsimd(out, ws_raw[h][:, :, lo : lo + P].rearrange("p t c -> p c t"))
+                    at += P
+            return tile
+
+        def passes(h, a, b):
+            x, i = divmod(h, HEADS)
+            bank = psum_bank([P, PACK, P], b)
+            first = (HEADS * a + i) * P
             for t in range(PACK):
                 matmul_mx(
-                    bank[:, t, :], w2_mx[h], h1_mx[h], slice(t * P, (t + 1) * P), slice(a * P, (a + 1) * P), True, True
+                    bank[:, t, :], w2_mx[h], h1_mx[x], slice(t * P, (t + 1) * P), slice(first, first + P), True, True
                 )
+            return bank
+
+        def evacuate(h, a, bank):
             nc.vector.tensor_tensor(
                 out=z_mx[h]["grouped"][:].rearrange("c (a r t) -> c a r t", a=A, t=PACK)[:, a, :, :],
                 in0=bank[:].rearrange("c t r -> c r t"),
@@ -160,32 +199,29 @@ def tile_treehopnode_pb_kernel(tc, h1, W2, b2, Ws, q, rep, out):
 
         out_banks = {}
 
-        def stage2(g, h):
+        def stage2(g, h, banks):
             width = COLUMN_GROUPS[g][1]
             for a in range(A):
                 if h == 0:
-                    out_banks[(g, a)] = psum_bank([P, width], 4 * (g % 2) + a)
+                    out_banks[(g, a)] = psum_bank([P, width], banks[a])
                 matmul_mx(
                     out_banks[(g, a)][:], z_mx[h], ws_mx[g][h], slice(a * P, (a + 1) * P), slice(0, width),
                     h == 0, h == H - 1,
                 )
 
-        def subtract(a):
-            nc.vector.tensor_tensor(out=residual[a][:], in0=q_raw[:, a, :], in1=rep_raw[:, a, :], op=SUBTRACT)
+        difference = {}
 
-        def subtract_by_tensor(a, first_bank):
-            banks = []
+        def subtract_on_tensor(a, first_bank):
             for c in range(2):
                 cols = slice(N_TILE * c, N_TILE * (c + 1))
                 bank = psum_bank([P, N_TILE], first_bank + c)
                 nc.tensor.matmul(bank[:], lhsT=identity_bf16[:], rhs=q_raw[:, a, cols], start=True, stop=False)
                 nc.tensor.matmul(bank[:], lhsT=minus_identity[:], rhs=rep_raw[:, a, cols], start=False, stop=True)
-                banks.append(bank)
-            return banks
+                difference[(a, c)] = bank
 
-        def copy_residual(a, banks):
+        def copy_residual(a):
             for c in range(2):
-                nc.scalar.copy(out=residual[a][:, N_TILE * c : N_TILE * (c + 1)], in_=banks[c][:])
+                nc.scalar.copy(out=residual[a][:, N_TILE * c : N_TILE * (c + 1)], in_=difference[(a, c)][:])
 
         out_by_tile = out.rearrange("(r a) e -> r a e", a=A)
 
@@ -197,77 +233,104 @@ def tile_treehopnode_pb_kernel(tc, h1, W2, b2, Ws, q, rep, out):
             )
             nc.sync.dma_start(out=out_by_tile[:, a, cols], in_=residual[a][:, cols])
 
-        regroup_w2(0, nc.vector.tensor_copy, 0, P // 2)
-        regroup_w2(0, nc.scalar.copy, P // 2, P)
+        regroup_w2(0, nc.vector.tensor_copy, 0, W2_VECTOR)
+        regroup_w2(0, nc.scalar.copy, W2_VECTOR, P)
         quantise(w2_mx[0])
-        warm_up = psum_bank([P, P], 0)
+        warm_up = psum_bank([P, P], 7)
         for i in range(4):
             nc.tensor.matmul(warm_up[:], lhsT=identity[:], rhs=identity[:], start=True, stop=True)
-        transpose_h1(0, 0)
-        transpose_bias(2)
-        quantise(h1_mx[0], 0, N_TILE // 2)
-        quantise(h1_mx[0], N_TILE // 2, N_TILE)
-        regroup_w2(1, nc.scalar.copy)
-        for a in range(A):
-            stage1(0, a)
-        transpose_h1(1, 0)
+        copy_h1(0, 0, transpose_h1(0, 0, 0))
+        copy_h1(0, 1, transpose_h1(0, 1, 1))
+        transpose_bias(4)
+        quantise(h1_mx[0], 0, 256)
+        quantise(h1_mx[0], 256, 512)
+        s0 = passes(0, 0, 4)
+        s1 = passes(0, 1, 5)
+        regroup_w2_shared(1, 3)
+        evacuate(0, 0, s0)
+        evacuate(0, 1, s1)
+        copy_h1(0, 2, transpose_h1(0, 2, 2))
+        copy_h1(0, 3, transpose_h1(0, 3, 3))
         quantise(w2_mx[1])
-        quantise(h1_mx[1])
+        regroup_w2_shared(2, 2)
+        s0 = passes(1, 0, 6)
+        s1 = passes(1, 1, 7)
+        for a in range(2):
+            copy_h1(1, a, transpose_h1(1, a, a))
+        regroup_w2_shared(3, 3, "w2_last")
+        evacuate(1, 0, s0)
+        quantise(h1_mx[0], 512, 1024)
+        evacuate(1, 1, s1)
+        s = [passes(h, a, 4 + 2 * h + a - 2) for h in range(2) for a in range(2, A)]
+        for h in range(2):
+            for a in range(2, A):
+                evacuate(h, a, s[2 * h + a - 2])
+        for a in range(2, A):
+            copy_h1(1, a, transpose_h1(1, a, a))
         quantise(z_mx[0])
-        prepare_head(2, 2)
-        for h in range(1, H):
-            stage1(h, 0)
-            stage1(h, 1)
-            if h + 1 < H:
-                quantise(w2_mx[h + 1])
-                if h > 1:
-                    quantise(z_mx[h - 1])
-                quantise(h1_mx[h + 1])
-            else:
-                quantise(z_mx[h - 1])
-                regroup_ws(0, 0)
-                quantise(ws_mx[0][0])
-            stage1(h, 2)
-            stage1(h, 3)
-            if h + 2 < H:
-                prepare_head(h + 2, 0)
-
+        quantise(h1_mx[1], 0, 512)
+        quantise(h1_mx[1], 512, 1024)
+        quantise(w2_mx[2])
+        quantise(z_mx[1])
+        regroup_ws(0, 0)
+        staged = regroup_ws_by_gpsimd(((2, 0, 0, 256), (2, 1, 0, 128)))
+        s = [passes(2, a, 4 + a) for a in range(2)]
+        s += [passes(2, a, 4 + a) for a in range(2, A)]
+        for a in range(A):
+            evacuate(2, a, s[a])
+        quantise(ws_mx[0][0])
+        quantise(w2_mx[3])
+        quantise(ws_mx[2][0], source=staged[:, :1024])
+        quantise(ws_mx[2][1], 0, 128, source=staged[:, 1024:1536])
+        staged = regroup_ws_by_gpsimd(((2, 2, 0, 256), (2, 1, 128, 128)))
         regroup_ws(0, 1)
-        quantise(ws_mx[0][1])
-        quantise(z_mx[H - 1])
-        stage2(0, 0)
-        stage2(0, 1)
-        banks0 = subtract_by_tensor(0, 4)
         regroup_ws(0, 2)
-        quantise(ws_mx[0][2])
-        stage2(0, 2)
+        s = [passes(3, a, a) for a in range(A)]
+        stage2(0, 0, (4, 5, 6, 7))
+        for a in range(A):
+            evacuate(3, a, s[a])
         regroup_ws(0, 3)
-        quantise(ws_mx[0][3])
-        stage2(0, 3)
+        subtract_on_tensor(0, 0)
+        subtract_on_tensor(1, 2)
+        copy_residual(0)
+        copy_residual(1)
+        quantise(ws_mx[0][1])
+        stage2(0, 1, None)
+        quantise(z_mx[2])
+        quantise(ws_mx[0][2])
+        stage2(0, 2, None)
+        subtract_on_tensor(2, 0)
         regroup_ws(1, 0)
-        quantise(ws_mx[1][0])
-        copy_residual(0, banks0)
-        subtract(1)
-        subtract(2)
+        copy_residual(2)
+        quantise(z_mx[3])
+        quantise(ws_mx[0][3])
+        stage2(0, 3, None)
+        nc.vector.tensor_tensor(out=residual[3][:], in0=q_raw[:, 3, :], in1=rep_raw[:, 3, :], op=SUBTRACT)
+        quantise(ws_mx[2][1], 128, 256, source=staged[:, 1024:1536])
+        quantise(ws_mx[2][2], source=staged[:, :1024])
+        staged = regroup_ws_by_gpsimd(((2, 3, 0, 256),))
         regroup_ws(1, 1)
+        for a in range(4):
+            finish(0, a)
+        quantise(ws_mx[1][0])
+        for a in range(4, A):
+            finish(0, a)
+        for h in range(3):
+            stage2(2, h, (0, 1, 2, 3))
+        quantise(ws_mx[2][3], source=staged[:, :1024])
+        stage2(2, 3, None)
         quantise(ws_mx[1][1])
-        subtract(3)
-        finish(0, 0)
+        for h in range(2):
+            stage2(1, h, (4, 5, 6, 7))
+        for a in range(2):
+            finish(2, a)
         regroup_ws(1, 2)
         quantise(ws_mx[1][2])
-        finish(0, 1)
-        finish(0, 2)
-        for h in range(3):
-            stage2(1, h)
+        stage2(1, 2, None)
+        for a in range(2, A):
+            finish(2, a)
         regroup_ws(1, 3)
         quantise(ws_mx[1][3])
-        stage2(1, 3)
-        finish(0, 3)
-        for g in range(2, len(COLUMN_GROUPS)):
-            for h in range(H):
-                regroup_ws(g, h)
-                quantise(ws_mx[g][h])
-                stage2(g, h)
-                finish(g - 1, h)
+        stage2(1, 3, None)
         for a in range(A):
-            finish(len(COLUMN_GROUPS) - 1, a)
+            finish(1, a)

@@ -65,9 +65,9 @@ def tile_treehopnode_pb_kernel(tc, h1, W2, b2, Ws, q, rep, out):
             )
 
         load_w2(0)
+        nc.sync.dma_start(out=bias_rows[:H, :], in_=b2)
         load_h1(0, 0, 1)
         load_h1(0, 1, 2)
-        nc.sync.dma_start(out=bias_rows[:H, :], in_=b2)
         load_w2(1)
         load_h1(0, 2, 4)
         load_w2(2)
@@ -236,60 +236,66 @@ def tile_treehopnode_pb_kernel(tc, h1, W2, b2, Ws, q, rep, out):
         regroup_w2(0, nc.vector.tensor_copy, 0, W2_VECTOR)
         regroup_w2(0, nc.scalar.copy, W2_VECTOR, P)
         quantise(w2_mx[0])
-        warm_up = psum_bank([P, P], 7)
-        for i in range(4):
-            nc.tensor.matmul(warm_up[:], lhsT=identity[:], rhs=identity[:], start=True, stop=True)
+        warm_up = psum_bank([P, P], 3)
+
+        def dummies(count):
+            for i in range(count):
+                nc.tensor.matmul(warm_up[:], lhsT=identity[:], rhs=identity[:], start=True, stop=True)
+
+        dummies(4)
+        transpose_bias(4)
         copy_h1(0, 0, transpose_h1(0, 0, 0))
         copy_h1(0, 1, transpose_h1(0, 1, 1))
-        transpose_bias(4)
+        dummies(1)
         quantise(h1_mx[0], 0, 256)
         quantise(h1_mx[0], 256, 512)
         s0 = passes(0, 0, 4)
+        dummies(1)
         s1 = passes(0, 1, 5)
-        regroup_w2_shared(1, 3)
+        regroup_w2_shared(1, 4)
         evacuate(0, 0, s0)
         evacuate(0, 1, s1)
         copy_h1(0, 2, transpose_h1(0, 2, 2))
-        copy_h1(0, 3, transpose_h1(0, 3, 3))
+        copy_h1(0, 3, transpose_h1(0, 3, 0))
         quantise(w2_mx[1])
-        regroup_w2_shared(2, 2)
+        regroup_w2_shared(2, 3)
         s0 = passes(1, 0, 6)
         s1 = passes(1, 1, 7)
-        for a in range(2):
-            copy_h1(1, a, transpose_h1(1, a, a))
+        copy_h1(1, 0, transpose_h1(1, 0, 1))
         regroup_w2_shared(3, 3, "w2_last")
         evacuate(1, 0, s0)
         quantise(h1_mx[0], 512, 1024)
         evacuate(1, 1, s1)
         s = [passes(h, a, 4 + 2 * h + a - 2) for h in range(2) for a in range(2, A)]
+        copy_h1(1, 1, transpose_h1(1, 1, 2))
         for h in range(2):
             for a in range(2, A):
                 evacuate(h, a, s[2 * h + a - 2])
         for a in range(2, A):
-            copy_h1(1, a, transpose_h1(1, a, a))
+            copy_h1(1, a, transpose_h1(1, a, (1 + a) % 3))
         quantise(z_mx[0])
         quantise(h1_mx[1], 0, 512)
         quantise(h1_mx[1], 512, 1024)
         quantise(w2_mx[2])
         quantise(z_mx[1])
         regroup_ws(0, 0)
-        staged = regroup_ws_by_gpsimd(((2, 0, 0, 256), (2, 1, 0, 128)))
-        s = [passes(2, a, 4 + a) for a in range(2)]
-        s += [passes(2, a, 4 + a) for a in range(2, A)]
+        staged = regroup_ws_by_gpsimd(((2, 0, 0, 256),))
+        s = [passes(2, a, 4 + a) for a in range(A)]
+        dummies(2)
         for a in range(A):
             evacuate(2, a, s[a])
         quantise(ws_mx[0][0])
         quantise(w2_mx[3])
         quantise(ws_mx[2][0], source=staged[:, :1024])
-        quantise(ws_mx[2][1], 0, 128, source=staged[:, 1024:1536])
-        staged = regroup_ws_by_gpsimd(((2, 2, 0, 256), (2, 1, 128, 128)))
+        staged = regroup_ws_by_gpsimd(((2, 2, 0, 256),))
         regroup_ws(0, 1)
         regroup_ws(0, 2)
-        s = [passes(3, a, a) for a in range(A)]
         stage2(0, 0, (4, 5, 6, 7))
+        s = [passes(3, a, a) for a in range(A)]
         for a in range(A):
             evacuate(3, a, s[a])
         regroup_ws(0, 3)
+        regroup_ws(2, 1)
         subtract_on_tensor(0, 0)
         subtract_on_tensor(1, 2)
         copy_residual(0)
@@ -306,15 +312,13 @@ def tile_treehopnode_pb_kernel(tc, h1, W2, b2, Ws, q, rep, out):
         quantise(ws_mx[0][3])
         stage2(0, 3, None)
         nc.vector.tensor_tensor(out=residual[3][:], in0=q_raw[:, 3, :], in1=rep_raw[:, 3, :], op=SUBTRACT)
-        quantise(ws_mx[2][1], 128, 256, source=staged[:, 1024:1536])
+        quantise(ws_mx[2][1])
         quantise(ws_mx[2][2], source=staged[:, :1024])
         staged = regroup_ws_by_gpsimd(((2, 3, 0, 256),))
         regroup_ws(1, 1)
-        for a in range(4):
+        for a in range(A):
             finish(0, a)
         quantise(ws_mx[1][0])
-        for a in range(4, A):
-            finish(0, a)
         for h in range(3):
             stage2(2, h, (0, 1, 2, 3))
         quantise(ws_mx[2][3], source=staged[:, :1024])
@@ -327,10 +331,10 @@ def tile_treehopnode_pb_kernel(tc, h1, W2, b2, Ws, q, rep, out):
         regroup_ws(1, 2)
         quantise(ws_mx[1][2])
         stage2(1, 2, None)
-        for a in range(2, A):
-            finish(2, a)
         regroup_ws(1, 3)
         quantise(ws_mx[1][3])
         stage2(1, 3, None)
+        for a in range(2, A):
+            finish(2, a)
         for a in range(A):
             finish(1, a)

@@ -252,8 +252,10 @@ def tile_treehopnode_pb_kernel(tc, h1, W2, b2, Ws, q, rep, out):
         s0 = passes(0, 0, 4)
         dummies(1)
         s1 = passes(0, 1, 5)
-        regroup_w2_shared(1, 4)
+        w2_mx[1]["grouped"] = sbuf.tile([P, N_TILE * PACK], BF16, name="w2_shared", tag="w2_shared", align_bytes=64)
+        regroup_w2(1, nc.scalar.copy, 0, 96)
         evacuate(0, 0, s0)
+        regroup_w2(1, nc.vector.tensor_copy, 96, P)
         evacuate(0, 1, s1)
         copy_h1(0, 2, transpose_h1(0, 2, 2))
         copy_h1(0, 3, transpose_h1(0, 3, 0))
@@ -262,7 +264,7 @@ def tile_treehopnode_pb_kernel(tc, h1, W2, b2, Ws, q, rep, out):
         s0 = passes(1, 0, 6)
         s1 = passes(1, 1, 7)
         copy_h1(1, 0, transpose_h1(1, 0, 1))
-        regroup_w2_shared(3, 3, "w2_last")
+        regroup_w2_shared(3, 2, "w2_last")
         evacuate(1, 0, s0)
         quantise(h1_mx[0], 512, 1024)
         evacuate(1, 1, s1)
@@ -284,14 +286,16 @@ def tile_treehopnode_pb_kernel(tc, h1, W2, b2, Ws, q, rep, out):
         dummies(2)
         for a in range(A):
             evacuate(2, a, s[a])
+        regroup_ws(0, 1)
         quantise(ws_mx[0][0])
         quantise(w2_mx[3])
+        quantise(ws_mx[0][1])
         quantise(ws_mx[2][0], source=staged[:, :1024])
         staged = regroup_ws_by_gpsimd(((2, 2, 0, 256),))
-        regroup_ws(0, 1)
         regroup_ws(0, 2)
         stage2(0, 0, (4, 5, 6, 7))
         s = [passes(3, a, a) for a in range(A)]
+        stage2(0, 1, None)
         for a in range(A):
             evacuate(3, a, s[a])
         regroup_ws(0, 3)
@@ -300,8 +304,6 @@ def tile_treehopnode_pb_kernel(tc, h1, W2, b2, Ws, q, rep, out):
         subtract_on_tensor(1, 2)
         copy_residual(0)
         copy_residual(1)
-        quantise(ws_mx[0][1])
-        stage2(0, 1, None)
         quantise(z_mx[2])
         quantise(ws_mx[0][2])
         stage2(0, 2, None)

from contextlib import ExitStack

import concourse.mybir as mybir
from concourse.masks import make_identity

FP8X4 = mybir.dt.float8_e4m3fn_x4
BF16 = mybir.dt.bfloat16
F32 = mybir.dt.float32
U32 = mybir.dt.uint32
U8 = mybir.dt.uint8
ADD = mybir.AluOpType.add
SUBTRACT = mybir.AluOpType.subtract
MULT = mybir.AluOpType.mult
HEADS = 2
W2_VECTOR = 80

P = 128
PACK = 4
N, E, G, M, H = 512, 1024, 512, 512, 4
A = N // P
N_TILE = 512
COLUMN_GROUPS = ((0, 512), (512, 256), (768, 256))
FLOPS = 2 * N * H * M * G + 2 * N * H * G * E


def tile_treehopnode_pb_kernel(tc, h1, W2, b2, Ws, q, rep, out):
    nc = tc.nc
    with ExitStack() as ctx:
        sbuf = ctx.enter_context(tc.tile_pool(name="sbuf", bufs=1))
        psum = ctx.enter_context(tc.psum_pool(name="psum", bufs=1))
        ctx.enter_context(tc.manual_schedule())

        identity = sbuf.tile([P, P], F32, name="identity")
        make_identity(nc, identity[:])
        identity_bf16 = sbuf.tile([P, P], BF16, name="identity_bf16")
        nc.scalar.copy(out=identity_bf16[:], in_=identity[:])
        minus_identity = sbuf.tile([P, P], BF16, name="minus_identity")
        nc.scalar.mul(out=minus_identity[:], in_=identity[:], mul=-1.0)
        bias = sbuf.tile([P, H, PACK], BF16, name="bias")
        bias_rows = sbuf.tile([P, G], BF16, name="bias_rows")
        nc.vector.memset(bias_rows[:], 0.0)

        h1_raw = [sbuf.tile([P, A, HEADS * M], BF16, name="h1_raw%d" % x) for x in range(H // HEADS)]
        w2_raw = [sbuf.tile([P, PACK, G], BF16, name="w2_raw%d" % h) for h in range(H)]
        ws_raw = [sbuf.tile([P, PACK, E], BF16, name="ws_raw%d" % h) for h in range(H)]
        q_raw = sbuf.tile([P, A, E], BF16, name="q_raw")
        rep_raw = sbuf.tile([P, A, E], BF16, name="rep_raw")
        h1_by_tile = h1.rearrange("(r a) (x i) m -> x r a (i m)", a=A, i=HEADS)
        q_by_tile = q.rearrange("(r a) e -> r a e", a=A)
        rep_by_tile = rep.rearrange("(r a) e -> r a e", a=A)

        def load_h1(x, first, last):
            nc.sync.dma_start(out=h1_raw[x][:, first:last, :], in_=h1_by_tile[x, :, first:last, :])

        def load_w2(h):
            nc.sync.dma_start(
                out=w2_raw[h][:].rearrange("p t g -> p (t g)"),
                in_=W2[h].rearrange("(p t) g -> p (t g)", t=PACK),
            )

        def load_ws(h):
            nc.sync.dma_start(
                out=ws_raw[h][:].rearrange("p t e -> p (t e)"),
                in_=Ws[h * G : (h + 1) * G, :].rearrange("(p t) e -> p (t e)", t=PACK),
            )

        load_w2(0)
        nc.sync.dma_start(out=bias_rows[:H, :], in_=b2)
        load_h1(0, 0, 1)
        load_h1(0, 1, 2)
        load_w2(1)
        load_h1(0, 2, 4)
        load_w2(2)
        load_h1(1, 0, 2)
        load_h1(1, 2, 4)
        load_w2(3)
        for h in range(H):
            load_ws(h)
        for b in range(2):
            tiles = slice(2 * b, 2 * b + 2)
            nc.sync.dma_start(out=q_raw[:, tiles, :], in_=q_by_tile[:, tiles, :])
            nc.sync.dma_start(out=rep_raw[:, tiles, :], in_=rep_by_tile[:, tiles, :])

        def mx_operand(name, width=512, grouped=True):
            return {
                "width": width,
                "grouped": sbuf.tile([P, width * PACK], BF16, name=name + "_grouped", align_bytes=64) if grouped else None,
                "words": sbuf.tile([P, width], U32, name=name + "_words", align_bytes=64),
                "scales": sbuf.tile([P, width], U8, name=name + "_scales", align_bytes=64),
            }

        h1_mx = [mx_operand("h1_%d" % x, A * HEADS * P) for x in range(H // HEADS)]
        w2_mx = [mx_operand("w2_%d" % h, grouped=h == 0) for h in range(H)]
        z_mx = [mx_operand("z_%d" % h) for h in range(H)]
        ws_mx = [
            [mx_operand("ws_%d_%d" % (first, h), width) for h in range(H)] for first, width in COLUMN_GROUPS
        ]
        residual = [sbuf.tile([P, E], F32, name="residual%d" % a) for a in range(A)]

        def quantise(operand, first=0, last=None, source=None):
            last = operand["width"] if last is None else last
            source = operand["grouped"][:, PACK * first : PACK * last] if source is None else source
            nc.vector.quantize_mx(
                out=operand["words"][:, first:last].bitcast(FP8X4),
                scales=operand["scales"][:, first:last],
                in_=source,
            )

        def matmul_mx(acc, stationary, moving, stationary_cols, moving_cols, start, stop):
            nc.tensor.matmul_mx(
                out=acc,
                lhsT=stationary["words"][:, stationary_cols].bitcast(FP8X4),
                lhsT_scale=stationary["scales"][:, stationary_cols],
                rhs=moving["words"][:, moving_cols].bitcast(FP8X4),
                rhs_scale=moving["scales"][:, moving_cols],
                start=start,
                stop=stop,
            )

        def psum_bank(shape, bank, dtype=F32):
            return psum.tile(shape, dtype, name="bank", tag="bank%d" % bank)

        def transpose_h1(x, a, b):
            pairs = h1_raw[x][:].rearrange("r a m -> r (a m)").bitcast(F32)
            bank = psum_bank([P, HEADS, 2, P], b)
            for i in range(HEADS):
                for u in range(2):
                    first = (M // 2) * (HEADS * a + i)
                    nc.tensor.transpose(bank[:, i, u, :], pairs[:, first + u : first + M // 2 : 2], identity[:])
            return bank

        def copy_h1(x, a, bank):
            grouped_pairs = h1_mx[x]["grouped"][:].bitcast(F32).rearrange("p (a i r u) -> p a i r u", a=A, i=HEADS, u=2)
            nc.scalar.copy(out=grouped_pairs[:, a], in_=bank[:].rearrange("p i u r -> p i r u"))

        def transpose_bias(bank):
            pairs = bias_rows[:].bitcast(F32)
            turned = psum_bank([P, 2, P], bank)
            for u in range(2):
                nc.tensor.transpose(turned[:, u, :], pairs[:, u::2], identity[:])
            nc.scalar.copy(
                out=bias[:].rearrange("c h t -> c (h t)").bitcast(F32).rearrange("c (h u) -> c h u", u=2),
                in_=turned[:, :, :H].rearrange("c u h -> c h u"),
            )

        def copy_by_gpsimd(out, in_):
            nc.gpsimd.tensor_scalar(out=out, in0=in_, scalar1=1.0, scalar2=0.0, op0=MULT, op1=ADD)

        def regroup_w2(h, copy, first=0, last=P):
            regrouped = w2_mx[h]["grouped"][:].rearrange("p (t c j) -> p c j t", t=PACK, j=PACK)
            rows = w2_raw[h][:].rearrange("p j (c t) -> p c j t", t=PACK)
            copy(out=regrouped[:, first:last], in_=rows[:, first:last])

        def regroup_w2_shared(h, split, tag="w2_shared"):
            w2_mx[h]["grouped"] = sbuf.tile([P, N_TILE * PACK], BF16, name="w2_shared", tag=tag, align_bytes=64)
            regrouped = w2_mx[h]["grouped"][:].rearrange("p (t c j) -> p t c j", t=PACK, j=PACK)
            rows = w2_raw[h][:].rearrange("p j (c t) -> p t c j", t=PACK)
            for t in range(split, PACK):
                copy_by_gpsimd(regrouped[:, t], rows[:, t])
            nc.scalar.copy(
                out=regrouped[:, :split].rearrange("p t c j -> p c j t"), in_=rows[:, :split].rearrange("p t c j -> p c j t")
            )

        def regroup_ws_by_gpsimd(pieces):
            tile = sbuf.tile([P, N_TILE * PACK], BF16, name="w2_shared", tag="w2_shared", align_bytes=64)
            at = 0
            for g, h, first, width in pieces:
                for k in range(0, width, P):
                    out = tile[:, PACK * at : PACK * (at + P)].rearrange("p (c t) -> p c t", t=PACK)
                    lo = COLUMN_GROUPS[g][0] + first + k
                    copy_by_gpsimd(out, ws_raw[h][:, :, lo : lo + P].rearrange("p t c -> p c t"))
                    at += P
            return tile

        def passes(h, a, b):
            x, i = divmod(h, HEADS)
            bank = psum_bank([P, PACK, P], b)
            first = (HEADS * a + i) * P
            for t in range(PACK):
                matmul_mx(
                    bank[:, t, :], w2_mx[h], h1_mx[x], slice(t * P, (t + 1) * P), slice(first, first + P), True, True
                )
            return bank

        def evacuate(h, a, bank):
            nc.vector.tensor_tensor(
                out=z_mx[h]["grouped"][:].rearrange("c (a r t) -> c a r t", a=A, t=PACK)[:, a, :, :],
                in0=bank[:].rearrange("c t r -> c r t"),
                in1=bias[:, h, :].unsqueeze(1).to_broadcast([P, P, PACK]),
                op=ADD,
            )

        def regroup_ws(g, h):
            first, width = COLUMN_GROUPS[g]
            nc.scalar.copy(
                out=ws_mx[g][h]["grouped"][:].rearrange("p (c i t) -> p c t i", i=4, t=PACK),
                in_=ws_raw[h][:, :, first : first + width].rearrange("p t (c i) -> p c t i", i=4),
            )

        out_banks = {}

        def stage2(g, h, banks):
            width = COLUMN_GROUPS[g][1]
            for a in range(A):
                if h == 0:
                    out_banks[(g, a)] = psum_bank([P, width], banks[a])
                matmul_mx(
                    out_banks[(g, a)][:], z_mx[h], ws_mx[g][h], slice(a * P, (a + 1) * P), slice(0, width),
                    h == 0, h == H - 1,
                )

        difference = {}

        def subtract_on_tensor(a, first_bank):
            for c in range(2):
                cols = slice(N_TILE * c, N_TILE * (c + 1))
                bank = psum_bank([P, N_TILE], first_bank + c)
                nc.tensor.matmul(bank[:], lhsT=identity_bf16[:], rhs=q_raw[:, a, cols], start=True, stop=False)
                nc.tensor.matmul(bank[:], lhsT=minus_identity[:], rhs=rep_raw[:, a, cols], start=False, stop=True)
                difference[(a, c)] = bank

        def copy_residual(a):
            for c in range(2):
                nc.scalar.copy(out=residual[a][:, N_TILE * c : N_TILE * (c + 1)], in_=difference[(a, c)][:])

        out_by_tile = out.rearrange("(r a) e -> r a e", a=A)

        def finish(g, a):
            first, width = COLUMN_GROUPS[g]
            cols = slice(first, first + width)
            nc.vector.tensor_tensor(
                out=residual[a][:, cols], in0=out_banks[(g, a)][:], in1=residual[a][:, cols], op=ADD
            )
            nc.sync.dma_start(out=out_by_tile[:, a, cols], in_=residual[a][:, cols])

        regroup_w2(0, nc.vector.tensor_copy, 0, W2_VECTOR)
        regroup_w2(0, nc.scalar.copy, W2_VECTOR, P)
        quantise(w2_mx[0])
        warm_up = psum_bank([P, P], 3)

        def dummies(count):
            for i in range(count):
                nc.tensor.matmul(warm_up[:], lhsT=identity[:], rhs=identity[:], start=True, stop=True)

        dummies(4)
        transpose_bias(4)
        copy_h1(0, 0, transpose_h1(0, 0, 0))
        copy_h1(0, 1, transpose_h1(0, 1, 1))
        dummies(1)
        quantise(h1_mx[0], 0, 256)
        quantise(h1_mx[0], 256, 512)
        s0 = passes(0, 0, 4)
        dummies(1)
        s1 = passes(0, 1, 5)
        w2_mx[1]["grouped"] = sbuf.tile([P, N_TILE * PACK], BF16, name="w2_shared", tag="w2_shared", align_bytes=64)
        regroup_w2(1, nc.scalar.copy, 0, 96)
        evacuate(0, 0, s0)
        regroup_w2(1, nc.vector.tensor_copy, 96, P)
        evacuate(0, 1, s1)
        copy_h1(0, 2, transpose_h1(0, 2, 2))
        copy_h1(0, 3, transpose_h1(0, 3, 0))
        quantise(w2_mx[1])
        regroup_w2_shared(2, 3)
        s0 = passes(1, 0, 6)
        s1 = passes(1, 1, 7)
        copy_h1(1, 0, transpose_h1(1, 0, 1))
        regroup_w2_shared(3, 2, "w2_last")
        evacuate(1, 0, s0)
        quantise(h1_mx[0], 512, 1024)
        evacuate(1, 1, s1)
        s = [passes(h, a, 4 + 2 * h + a - 2) for h in range(2) for a in range(2, A)]
        copy_h1(1, 1, transpose_h1(1, 1, 2))
        for h in range(2):
            for a in range(2, A):
                evacuate(h, a, s[2 * h + a - 2])
        for a in range(2, A):
            copy_h1(1, a, transpose_h1(1, a, (1 + a) % 3))
        quantise(z_mx[0])
        quantise(h1_mx[1], 0, 512)
        quantise(h1_mx[1], 512, 1024)
        quantise(w2_mx[2])
        quantise(z_mx[1])
        regroup_ws(0, 0)
        staged = regroup_ws_by_gpsimd(((2, 0, 0, 256),))
        s = [passes(2, a, 4 + a) for a in range(A)]
        dummies(2)
        for a in range(A):
            evacuate(2, a, s[a])
        regroup_ws(0, 1)
        quantise(ws_mx[0][0])
        quantise(w2_mx[3])
        quantise(ws_mx[0][1])
        quantise(ws_mx[2][0], source=staged[:, :1024])
        staged = regroup_ws_by_gpsimd(((2, 2, 0, 256),))
        regroup_ws(0, 2)
        stage2(0, 0, (4, 5, 6, 7))
        s = [passes(3, a, a) for a in range(A)]
        stage2(0, 1, None)
        for a in range(A):
            evacuate(3, a, s[a])
        regroup_ws(0, 3)
        regroup_ws(2, 1)
        subtract_on_tensor(0, 0)
        subtract_on_tensor(1, 2)
        copy_residual(0)
        copy_residual(1)
        quantise(z_mx[2])
        quantise(ws_mx[0][2])
        stage2(0, 2, None)
        subtract_on_tensor(2, 0)
        regroup_ws(1, 0)
        copy_residual(2)
        quantise(z_mx[3])
        quantise(ws_mx[0][3])
        stage2(0, 3, None)
        nc.vector.tensor_tensor(out=residual[3][:], in0=q_raw[:, 3, :], in1=rep_raw[:, 3, :], op=SUBTRACT)
        quantise(ws_mx[2][1])
        quantise(ws_mx[2][2], source=staged[:, :1024])
        staged = regroup_ws_by_gpsimd(((2, 3, 0, 256),))
        regroup_ws(1, 1)
        for a in range(A):
            finish(0, a)
        quantise(ws_mx[1][0])
        for h in range(3):
            stage2(2, h, (0, 1, 2, 3))
        quantise(ws_mx[2][3], source=staged[:, :1024])
        stage2(2, 3, None)
        quantise(ws_mx[1][1])
        for h in range(2):
            stage2(1, h, (4, 5, 6, 7))
        for a in range(2):
            finish(2, a)
        regroup_ws(1, 2)
        quantise(ws_mx[1][2])
        stage2(1, 2, None)
        regroup_ws(1, 3)
        quantise(ws_mx[1][3])
        stage2(1, 3, None)
        for a in range(2, A):
            finish(2, a)
        for a in range(A):
            finish(1, a)
